import numpy as np
import ml_dtypes


def mxq(x, axis, fmt="e4m3"):
    dtype, down = {"e4m3": (ml_dtypes.float8_e4m3fn, 7), "e5m2": (ml_dtypes.float8_e5m2, 14)}[fmt]
    v = np.moveaxis(np.asarray(x, np.float32).astype(ml_dtypes.bfloat16).astype(np.float64), axis, -1)
    blocks = v.reshape(v.shape[:-1] + (-1, 32))
    amax = np.abs(blocks).max(-1, keepdims=True)
    byte = np.maximum(np.where(amax > 0, np.frexp(amax)[1] - 1 + 127, 0) - down, 1)
    scale = np.exp2(byte - 127.0)
    codes = (blocks / scale).astype(np.float32).astype(dtype).astype(np.float64)
    return np.moveaxis((codes * scale).reshape(v.shape), -1, axis)


WIDE = False


def mx_kscale(k):
    if not WIDE:
        return np.ones(k)
    levels = np.array([20, -20, 10, -10, 0])
    a = np.random.permutation(np.resize(levels, k // 512 * 4)).reshape(k // 512, 4)
    idx = np.arange(k)
    return np.exp2(a[idx // 512, idx % 128 // 32])


BF16 = ml_dtypes.bfloat16


def bf(x):
    return np.asarray(x, np.float32).astype(BF16)


def f64(x):
    return np.asarray(x).astype(np.float64)


N, P, D, E, F = 512, 3, 128, 8192, 1024


def setup_inputs():
    u = mx_kscale(E)
    x = np.random.standard_normal((N, P, D)) + 0.5 * np.random.standard_normal((1, P, D))
    w1a = np.random.standard_normal((D, E)) / np.sqrt(D) / u[None, :]
    w2a = np.random.standard_normal((D, E)) / np.sqrt(D) / u[None, :]
    g = np.random.standard_normal((N, P, E)) * np.exp2(np.random.randint(-12, 1, (N, P, 1))) * 4.0 * u
    return {"x": bf(x), "w1a": bf(w1a), "w2a": bf(w2a), "grad_out": bf(g)}


def reference(x, w1a, w2a, grad_out):
    gq = mxq(f64(grad_out), 2, "e5m2")
    a = gq @ mxq(f64(w2a), 1, "e4m3").T
    b = gq @ mxq(f64(w1a), 1, "e4m3").T
    return a + (b.sum(axis=1, keepdims=True) - b) * 0.5

@@ -1,0 +1,161 @@
+from contextlib import ExitStack
+
+import concourse.mybir as mybir
+from concourse.masks import make_identity
+
+F32 = mybir.dt.float32
+BF16 = mybir.dt.bfloat16
+U32 = mybir.dt.uint32
+U8 = mybir.dt.uint8
+E5M2_X4 = mybir.dt.float8_e5m2_x4
+E4M3_X4 = mybir.dt.float8_e4m3fn_x4
+MULT = mybir.AluOpType.mult
+ADD = mybir.AluOpType.add
+
+ITEMS, HOPS, D, E = 512, 3, 128, 8192
+P = 128
+PACK = 4
+K_PASS = P * PACK
+PASSES = E // K_PASS
+HALVES = 2
+WORDS = K_PASS // 2
+ITEM_TILES = ITEMS // P
+LOAD_PASSES = 4
+LOAD_K = LOAD_PASSES * K_PASS
+LOADS = PASSES // LOAD_PASSES
+ROUND_PASSES = 2
+AHEAD = 5
+
+FLOPS = 2 * 2 * ITEMS * HOPS * E * D
+BYTES = 2 * ITEMS * HOPS * E + 2 * 2 * D * E + 4 * ITEMS * HOPS * D
+
+
+def tile_dogtaitujuanji_pa_k_kernel(tc, x, w1a, w2a, grad_out, out):
+    nc = tc.nc
+    with ExitStack() as ctx:
+        ctx.enter_context(tc.manual_schedule())
+        keep = ctx.enter_context(tc.tile_pool(name="keep", bufs=1))
+        w_raw_pool = ctx.enter_context(tc.tile_pool(name="w_raw", bufs=2 * LOADS))
+        g_raw_pool = ctx.enter_context(tc.tile_pool(name="g_raw", bufs=ITEM_TILES * (AHEAD + 1)))
+        w_stage = ctx.enter_context(tc.tile_pool(name="w_stage", bufs=2))
+        g_stage = ctx.enter_context(tc.tile_pool(name="g_stage", bufs=2 * ROUND_PASSES))
+        out_stage = ctx.enter_context(tc.tile_pool(name="out_stage", bufs=ITEM_TILES))
+        acc_pool = ctx.enter_context(tc.psum_pool(name="acc", bufs=1))
+        bank_pool = ctx.enter_context(tc.psum_pool(name="banks", bufs=6))
+
+        ident = keep.tile([P, P], F32)
+        make_identity(nc, ident[:])
+        mix = keep.tile([P, HOPS, ITEMS], F32)
+        nc.vector.memset(mix[:], 0.0)
+        w_codes = keep.tile([P, PASSES, 2 * D], U32, align_bytes=64)
+        w_scales = keep.tile([P, PASSES, 2 * D], U8, align_bytes=64)
+
+        g_rows = grad_out.rearrange("(t p) h k -> h t p k", p=P)
+        w_raw = {}
+        g_raw = {}
+        acc = {}
+
+        def load_step(hop, load):
+            k_cols = slice(load * LOAD_K, (load + 1) * LOAD_K)
+            if hop == 0:
+                for which, w in enumerate((w2a, w1a)):
+                    w_piece = w_raw_pool.tile([P, LOAD_K], BF16, tag="w_raw", name="w_piece")
+                    nc.sync.dma_start(out=w_piece[:], in_=w[:, k_cols])
+                    w_raw[(which, load)] = w_piece
+            for t in range(ITEM_TILES):
+                g_piece = g_raw_pool.tile([P, LOAD_K], BF16, tag="g_raw", name="g_piece")
+                nc.sync.dma_start(out=g_piece[:], in_=g_rows[hop, t, :, k_cols])
+                g_raw[(hop, load, t)] = g_piece
+
+        def transpose_words(bank_cols, piece, pass_in_load, u):
+            first = WORDS * pass_in_load + P * u
+            nc.tensor.transpose(bank_cols, piece[:].bitcast(F32)[:, first : first + P], ident[:])
+
+        def quantise_weights(load):
+            grouped = w_stage.tile([P, LOAD_PASSES * 2 * D * PACK], BF16, align_bytes=64, tag="w_grouped", name="w_grouped")
+            grouped_words = grouped[:].bitcast(F32).rearrange("p (c m u) -> p c m u", c=LOAD_PASSES, u=HALVES)
+            for c in range(LOAD_PASSES):
+                bank = bank_pool.tile([P, HALVES, 2 * D], F32, tag="bank", name="w_bank")
+                for which in range(2):
+                    for u in range(HALVES):
+                        transpose_words(bank[:, u, D * which : D * (which + 1)], w_raw[(which, load)], c, u)
+                empty = nc.vector.tensor_copy if c % 2 == 0 else nc.scalar.copy
+                empty(out=grouped_words[:, c, :, :], in_=bank[:].rearrange("p u m -> p m u"))
+            passes = slice(load * LOAD_PASSES, (load + 1) * LOAD_PASSES)
+            nc.vector.quantize_mx(
+                out=w_codes[:, passes, :].rearrange("p c m -> p (c m)").bitcast(E4M3_X4),
+                scales=w_scales[:, passes, :].rearrange("p c m -> p (c m)"),
+                in_=grouped[:],
+            )
+
+        def quantise_round(hop, first_pass):
+            operands = []
+            for c in range(first_pass, first_pass + ROUND_PASSES):
+                load, pass_in_load = divmod(c, LOAD_PASSES)
+                grouped = g_stage.tile([P, ITEMS * PACK], BF16, align_bytes=64, tag="g_grouped", name="g_grouped")
+                grouped_words = grouped[:].bitcast(F32).rearrange("p (n u) -> p n u", u=HALVES)
+                for pair in range(ITEM_TILES // 2):
+                    bank = bank_pool.tile([P, HALVES, 2 * P], F32, tag="bank", name="g_bank")
+                    for j in range(2):
+                        for u in range(HALVES):
+                            transpose_words(bank[:, u, P * j : P * (j + 1)], g_raw[(hop, load, 2 * pair + j)], pass_in_load, u)
+                    empty = nc.vector.tensor_copy if (c == first_pass and pair == 0) else nc.scalar.copy
+                    empty(out=grouped_words[:, 2 * P * pair : 2 * P * (pair + 1), :], in_=bank[:].rearrange("p u n -> p n u"))
+                g_codes = g_stage.tile([P, ITEMS], U32, align_bytes=64, tag="g_codes", name="g_codes")
+                g_scales = g_stage.tile([P, ITEMS], U8, align_bytes=64, tag="g_scales", name="g_scales")
+                nc.vector.quantize_mx(out=g_codes[:].bitcast(E5M2_X4), scales=g_scales[:], in_=grouped[:])
+                operands.append((hop, c, g_codes, g_scales))
+            return operands
+
+        def finish_hop(hop):
+            b_sb = out_stage.tile([P, ITEMS], F32, tag="b_sb", name="b_sb", bufs=1)
+            nc.scalar.copy(out=b_sb[:], in_=acc["b"][:])
+            nc.vector.tensor_add(out=mix[:, hop, :], in0=mix[:, hop, :], in1=acc["a"][:])
+            for other in range(HOPS):
+                if other != hop:
+                    nc.vector.scalar_tensor_tensor(
+                        out=mix[:, other, :], in0=b_sb[:], scalar=0.5, in1=mix[:, other, :], op0=MULT, op1=ADD
+                    )
+
+        def multiply_round(operands):
+            for hop, c, g_codes, g_scales in operands:
+                if c == 0:
+                    acc["a"] = acc_pool.tile([P, ITEMS], F32, tag="acc_a", name="acc_a")
+                    acc["b"] = acc_pool.tile([P, ITEMS], F32, tag="acc_b", name="acc_b")
+                for which, key in enumerate(("a", "b")):
+                    nc.tensor.matmul_mx(
+                        out=acc[key][:],
+                        lhsT=w_codes[:, c, D * which : D * (which + 1)].bitcast(E4M3_X4),
+                        lhsT_scale=w_scales[:, c, D * which : D * (which + 1)],
+                        rhs=g_codes[:].bitcast(E5M2_X4),
+                        rhs_scale=g_scales[:],
+                        start=(c == 0),
+                        stop=(c == PASSES - 1),
+                    )
+                if c == PASSES - 1:
+                    finish_hop(hop)
+
+        steps = [(hop, load) for hop in range(HOPS) for load in range(LOADS)]
+        for hop, load in steps[:AHEAD]:
+            load_step(hop, load)
+        waiting = []
+        for s, (hop, load) in enumerate(steps):
+            if s + AHEAD < len(steps):
+                load_step(*steps[s + AHEAD])
+            if hop == 0:
+                quantise_weights(load)
+            for first_pass in range(load * LOAD_PASSES, (load + 1) * LOAD_PASSES, ROUND_PASSES):
+                quantised = quantise_round(hop, first_pass)
+                multiply_round(waiting)
+                waiting = quantised
+        multiply_round(waiting)
+
+        out_rows = out.rearrange("(t p) h d -> t p h d", p=P)
+        for t in range(ITEM_TILES):
+            out_bank = bank_pool.tile([P, HOPS, D], F32, tag="bank", name="out_bank")
+            for hop in range(HOPS):
+                nc.tensor.transpose(out_bank[:, hop, :], mix[:, hop, P * t : P * (t + 1)], ident[:])
+            out_sb = out_stage.tile([P, HOPS, D], F32, tag="out_sb", name="out_sb")
+            empty = nc.vector.tensor_copy if t % 2 == 0 else nc.scalar.copy
+            empty(out=out_sb[:], in_=out_bank[:])
+            nc.sync.dma_start(out=out_rows[t], in_=out_sb[:])

@@ -20,11 +20,11 @@ PASSES = E // K_PASS
 HALVES = 2
 WORDS = K_PASS // 2
 ITEM_TILES = ITEMS // P
-LOAD_PASSES = 4
-LOAD_K = LOAD_PASSES * K_PASS
-LOADS = PASSES // LOAD_PASSES
-ROUND_PASSES = 2
+ROUND_PASSES = 4
+ROUND_K = ROUND_PASSES * K_PASS
+ROUNDS = PASSES // ROUND_PASSES
 AHEAD = 5
+BANKS = 6
 
 FLOPS = 2 * 2 * ITEMS * HOPS * E * D
 BYTES = 2 * ITEMS * HOPS * E + 2 * 2 * D * E + 4 * ITEMS * HOPS * D
@@ -35,13 +35,14 @@ def tile_dogtaitujuanji_pa_k_kernel(tc, x, w1a, w2a, grad_out, out):
     with ExitStack() as ctx:
         ctx.enter_context(tc.manual_schedule())
         keep = ctx.enter_context(tc.tile_pool(name="keep", bufs=1))
-        w_raw_pool = ctx.enter_context(tc.tile_pool(name="w_raw", bufs=2 * LOADS))
+        w_raw_pool = ctx.enter_context(tc.tile_pool(name="w_raw", bufs=2 * ROUNDS))
         g_raw_pool = ctx.enter_context(tc.tile_pool(name="g_raw", bufs=ITEM_TILES * (AHEAD + 1)))
-        w_stage = ctx.enter_context(tc.tile_pool(name="w_stage", bufs=2))
-        g_stage = ctx.enter_context(tc.tile_pool(name="g_stage", bufs=2 * ROUND_PASSES))
+        grouped_pool = ctx.enter_context(tc.tile_pool(name="grouped", bufs=ROUND_PASSES))
+        w_grouped_pool = ctx.enter_context(tc.tile_pool(name="w_grouped", bufs=2))
+        operand_pool = ctx.enter_context(tc.tile_pool(name="operands", bufs=2 * ROUND_PASSES))
         out_stage = ctx.enter_context(tc.tile_pool(name="out_stage", bufs=ITEM_TILES))
         acc_pool = ctx.enter_context(tc.psum_pool(name="acc", bufs=1))
-        bank_pool = ctx.enter_context(tc.psum_pool(name="banks", bufs=6))
+        bank_pool = ctx.enter_context(tc.psum_pool(name="banks", bufs=BANKS))
 
         ident = keep.tile([P, P], F32)
         make_identity(nc, ident[:])
@@ -55,74 +56,66 @@ def tile_dogtaitujuanji_pa_k_kernel(tc, x, w1a, w2a, grad_out, out):
         g_raw = {}
         acc = {}
 
-        def load_step(hop, load):
-            k_cols = slice(load * LOAD_K, (load + 1) * LOAD_K)
+        def load_round(hop, r):
+            k_cols = slice(r * ROUND_K, (r + 1) * ROUND_K)
             if hop == 0:
                 for which, w in enumerate((w2a, w1a)):
-                    w_piece = w_raw_pool.tile([P, LOAD_K], BF16, tag="w_raw", name="w_piece")
+                    w_piece = w_raw_pool.tile([P, ROUND_K], BF16, tag="w_raw", name="w_piece")
                     nc.sync.dma_start(out=w_piece[:], in_=w[:, k_cols])
-                    w_raw[(which, load)] = w_piece
+                    w_raw[(which, r)] = w_piece
             for t in range(ITEM_TILES):
-                g_piece = g_raw_pool.tile([P, LOAD_K], BF16, tag="g_raw", name="g_piece")
+                g_piece = g_raw_pool.tile([P, ROUND_K], BF16, tag="g_raw", name="g_piece")
                 nc.sync.dma_start(out=g_piece[:], in_=g_rows[hop, t, :, k_cols])
-                g_raw[(hop, load, t)] = g_piece
+                g_raw[(hop, r, t)] = g_piece
 
-        def transpose_words(bank_cols, piece, pass_in_load, u):
-            first = WORDS * pass_in_load + P * u
+        def transpose_words(bank_cols, piece, c, u):
+            first = WORDS * c + P * u
             nc.tensor.transpose(bank_cols, piece[:].bitcast(F32)[:, first : first + P], ident[:])
 
-        def quantise_weights(load):
-            grouped = w_stage.tile([P, LOAD_PASSES * 2 * D * PACK], BF16, align_bytes=64, tag="w_grouped", name="w_grouped")
-            grouped_words = grouped[:].bitcast(F32).rearrange("p (c m u) -> p c m u", c=LOAD_PASSES, u=HALVES)
-            for c in range(LOAD_PASSES):
+        def transpose_weights(r):
+            grouped = w_grouped_pool.tile([P, ROUND_PASSES * 2 * D * PACK], BF16, align_bytes=64, tag="w_grouped", name="w_grouped")
+            grouped_words = grouped[:].bitcast(F32).rearrange("p (c m u) -> p c m u", c=ROUND_PASSES, u=HALVES)
+            for c in range(ROUND_PASSES):
                 bank = bank_pool.tile([P, HALVES, 2 * D], F32, tag="bank", name="w_bank")
                 for which in range(2):
                     for u in range(HALVES):
-                        transpose_words(bank[:, u, D * which : D * (which + 1)], w_raw[(which, load)], c, u)
+                        transpose_words(bank[:, u, D * which : D * (which + 1)], w_raw[(which, r)], c, u)
                 empty = nc.vector.tensor_copy if c % 2 == 0 else nc.scalar.copy
                 empty(out=grouped_words[:, c, :, :], in_=bank[:].rearrange("p u m -> p m u"))
-            passes = slice(load * LOAD_PASSES, (load + 1) * LOAD_PASSES)
+            return grouped
+
+        def quantise_weights(r, grouped):
+            passes = slice(r * ROUND_PASSES, (r + 1) * ROUND_PASSES)
             nc.vector.quantize_mx(
                 out=w_codes[:, passes, :].rearrange("p c m -> p (c m)").bitcast(E4M3_X4),
                 scales=w_scales[:, passes, :].rearrange("p c m -> p (c m)"),
                 in_=grouped[:],
             )
 
-        def quantise_round(hop, first_pass):
+        def quantise_round(hop, r):
             operands = []
-            for c in range(first_pass, first_pass + ROUND_PASSES):
-                load, pass_in_load = divmod(c, LOAD_PASSES)
-                grouped = g_stage.tile([P, ITEMS * PACK], BF16, align_bytes=64, tag="g_grouped", name="g_grouped")
+            for c in range(ROUND_PASSES):
+                grouped = grouped_pool.tile([P, ITEMS * PACK], BF16, align_bytes=64, tag="g_grouped", name="g_grouped")
                 grouped_words = grouped[:].bitcast(F32).rearrange("p (n u) -> p n u", u=HALVES)
                 for pair in range(ITEM_TILES // 2):
                     bank = bank_pool.tile([P, HALVES, 2 * P], F32, tag="bank", name="g_bank")
                     for j in range(2):
                         for u in range(HALVES):
-                            transpose_words(bank[:, u, P * j : P * (j + 1)], g_raw[(hop, load, 2 * pair + j)], pass_in_load, u)
-                    empty = nc.vector.tensor_copy if (c == first_pass and pair == 0) else nc.scalar.copy
+                            transpose_words(bank[:, u, P * j : P * (j + 1)], g_raw[(hop, r, 2 * pair + j)], c, u)
+                    empty = nc.vector.tensor_copy if (c % 2 == 0 and pair == 0) else nc.scalar.copy
                     empty(out=grouped_words[:, 2 * P * pair : 2 * P * (pair + 1), :], in_=bank[:].rearrange("p u n -> p n u"))
-                g_codes = g_stage.tile([P, ITEMS], U32, align_bytes=64, tag="g_codes", name="g_codes")
-                g_scales = g_stage.tile([P, ITEMS], U8, align_bytes=64, tag="g_scales", name="g_scales")
+                g_codes = operand_pool.tile([P, ITEMS], U32, align_bytes=64, tag="g_codes", name="g_codes")
+                g_scales = operand_pool.tile([P, ITEMS], U8, align_bytes=64, tag="g_scales", name="g_scales")
                 nc.vector.quantize_mx(out=g_codes[:].bitcast(E5M2_X4), scales=g_scales[:], in_=grouped[:])
-                operands.append((hop, c, g_codes, g_scales))
+                operands.append((r * ROUND_PASSES + c, g_codes, g_scales))
             return operands
 
-        def finish_hop(hop):
-            b_sb = out_stage.tile([P, ITEMS], F32, tag="b_sb", name="b_sb", bufs=1)
-            nc.scalar.copy(out=b_sb[:], in_=acc["b"][:])
-            nc.vector.tensor_add(out=mix[:, hop, :], in0=mix[:, hop, :], in1=acc["a"][:])
-            for other in range(HOPS):
-                if other != hop:
-                    nc.vector.scalar_tensor_tensor(
-                        out=mix[:, other, :], in0=b_sb[:], scalar=0.5, in1=mix[:, other, :], op0=MULT, op1=ADD
-                    )
-
-        def multiply_round(operands):
-            for hop, c, g_codes, g_scales in operands:
-                if c == 0:
-                    acc["a"] = acc_pool.tile([P, ITEMS], F32, tag="acc_a", name="acc_a")
-                    acc["b"] = acc_pool.tile([P, ITEMS], F32, tag="acc_b", name="acc_b")
-                for which, key in enumerate(("a", "b")):
+        def multiply_round(hop, operands):
+            if operands[0][0] == 0:
+                acc["a"] = acc_pool.tile([P, ITEMS], F32, tag="acc_a", name="acc_a")
+                acc["b"] = acc_pool.tile([P, ITEMS], F32, tag="acc_b", name="acc_b")
+            for key, which in (("b", 1), ("a", 0)):
+                for c, g_codes, g_scales in operands:
                     nc.tensor.matmul_mx(
                         out=acc[key][:],
                         lhsT=w_codes[:, c, D * which : D * (which + 1)].bitcast(E4M3_X4),
@@ -132,23 +125,35 @@ def tile_dogtaitujuanji_pa_k_kernel(tc, x, w1a, w2a, grad_out, out):
                         start=(c == 0),
                         stop=(c == PASSES - 1),
                     )
-                if c == PASSES - 1:
-                    finish_hop(hop)
+            if operands[-1][0] == PASSES - 1:
+                finish_hop(hop)
 
-        steps = [(hop, load) for hop in range(HOPS) for load in range(LOADS)]
-        for hop, load in steps[:AHEAD]:
-            load_step(hop, load)
-        waiting = []
-        for s, (hop, load) in enumerate(steps):
-            if s + AHEAD < len(steps):
-                load_step(*steps[s + AHEAD])
+        def finish_hop(hop):
+            b_sb = out_stage.tile([P, ITEMS], F32, tag="b_sb", name="b_sb", bufs=1)
+            nc.scalar.copy(out=b_sb[:], in_=acc["b"][:])
+            for other in range(HOPS):
+                if other != hop:
+                    nc.vector.scalar_tensor_tensor(
+                        out=mix[:, other, :], in0=b_sb[:], scalar=0.5, in1=mix[:, other, :], op0=MULT, op1=ADD
+                    )
+            nc.vector.tensor_add(out=mix[:, hop, :], in0=mix[:, hop, :], in1=acc["a"][:])
+
+        rounds = [(hop, r) for hop in range(HOPS) for r in range(ROUNDS)]
+        for hop, r in rounds[:AHEAD]:
+            load_round(hop, r)
+        waiting = None
+        for i, (hop, r) in enumerate(rounds):
+            if i + AHEAD < len(rounds):
+                load_round(*rounds[i + AHEAD])
             if hop == 0:
-                quantise_weights(load)
-            for first_pass in range(load * LOAD_PASSES, (load + 1) * LOAD_PASSES, ROUND_PASSES):
-                quantised = quantise_round(hop, first_pass)
-                multiply_round(waiting)
-                waiting = quantised
-        multiply_round(waiting)
+                w_grouped = transpose_weights(r)
+            operands = quantise_round(hop, r)
+            if hop == 0:
+                quantise_weights(r, w_grouped)
+            if waiting is not None:
+                multiply_round(*waiting)
+            waiting = (hop, operands)
+        multiply_round(*waiting)
 
         out_rows = out.rearrange("(t p) h d -> t p h d", p=P)
         for t in range(ITEM_TILES):

@@ -33,7 +33,6 @@ BYTES = 2 * ITEMS * HOPS * E + 2 * 2 * D * E + 4 * ITEMS * HOPS * D
 def tile_dogtaitujuanji_pa_k_kernel(tc, x, w1a, w2a, grad_out, out):
     nc = tc.nc
     with ExitStack() as ctx:
-        ctx.enter_context(tc.manual_schedule())
         keep = ctx.enter_context(tc.tile_pool(name="keep", bufs=1))
         w_raw_pool = ctx.enter_context(tc.tile_pool(name="w_raw", bufs=2 * ROUNDS))
         g_raw_pool = ctx.enter_context(tc.tile_pool(name="g_raw", bufs=ITEM_TILES * (AHEAD + 1)))

@@ -11,6 +11,7 @@ E5M2_X4 = mybir.dt.float8_e5m2_x4
 E4M3_X4 = mybir.dt.float8_e4m3fn_x4
 MULT = mybir.AluOpType.mult
 ADD = mybir.AluOpType.add
+COPY = mybir.ActivationFunctionType.Copy
 
 ITEMS, HOPS, D, E = 512, 3, 128, 8192
 P = 128
@@ -25,6 +26,7 @@ ROUND_K = ROUND_PASSES * K_PASS
 ROUNDS = PASSES // ROUND_PASSES
 AHEAD = 5
 BANKS = 6
+WARM_UP = 4
 
 FLOPS = 2 * 2 * ITEMS * HOPS * E * D
 BYTES = 2 * ITEMS * HOPS * E + 2 * 2 * D * E + 4 * ITEMS * HOPS * D
@@ -43,14 +45,19 @@ def tile_dogtaitujuanji_pa_k_kernel(tc, x, w1a, w2a, grad_out, out):
         acc_pool = ctx.enter_context(tc.psum_pool(name="acc", bufs=1))
         bank_pool = ctx.enter_context(tc.psum_pool(name="banks", bufs=BANKS))
 
+        zeros = keep.tile([P, ITEMS], BF16)
+        nc.vector.memset(zeros[:], 0.0)
+        warm_bank = bank_pool.tile([P, ITEMS], F32, tag="bank", name="warm_bank")
+        for i in range(WARM_UP):
+            nc.tensor.matmul(warm_bank[:], lhsT=zeros[:, :P], rhs=zeros[:], start=True, stop=True)
         ident = keep.tile([P, P], F32)
         make_identity(nc, ident[:])
         mix = keep.tile([P, HOPS, ITEMS], F32)
-        nc.vector.memset(mix[:], 0.0)
         w_codes = keep.tile([P, PASSES, 2 * D], U32, align_bytes=64)
         w_scales = keep.tile([P, PASSES, 2 * D], U8, align_bytes=64)
 
         g_rows = grad_out.rearrange("(t p) h k -> h t p k", p=P)
+        out_rows = out.rearrange("(t p) h d -> t p h d", p=P)
         w_raw = {}
         g_raw = {}
         acc = {}
@@ -128,14 +135,34 @@ def tile_dogtaitujuanji_pa_k_kernel(tc, x, w1a, w2a, grad_out, out):
                 finish_hop(hop)
 
         def finish_hop(hop):
-            b_sb = out_stage.tile([P, ITEMS], F32, tag="b_sb", name="b_sb", bufs=1)
-            nc.scalar.copy(out=b_sb[:], in_=acc["b"][:])
-            for other in range(HOPS):
-                if other != hop:
-                    nc.vector.scalar_tensor_tensor(
-                        out=mix[:, other, :], in0=b_sb[:], scalar=0.5, in1=mix[:, other, :], op0=MULT, op1=ADD
-                    )
-            nc.vector.tensor_add(out=mix[:, hop, :], in0=mix[:, hop, :], in1=acc["a"][:])
+            others = [other for other in range(HOPS) if other != hop]
+            if hop == 0:
+                for other in others:
+                    nc.scalar.activation(out=mix[:, other, :], in_=acc["b"][:], func=COPY, scale=0.5)
+                nc.scalar.copy(out=mix[:, hop, :], in_=acc["a"][:])
+                return
+            for other in others:
+                nc.vector.scalar_tensor_tensor(
+                    out=mix[:, other, :], in0=acc["b"][:], scalar=0.5, in1=mix[:, other, :], op0=MULT, op1=ADD
+                )
+            if hop < HOPS - 1:
+                nc.vector.tensor_add(out=mix[:, hop, :], in0=mix[:, hop, :], in1=acc["a"][:])
+                return
+            out_banks = []
+            for t in range(ITEM_TILES):
+                out_bank = bank_pool.tile([P, HOPS, D], F32, tag="bank", name="out_bank")
+                for other in others:
+                    nc.tensor.transpose(out_bank[:, other, :], mix[:, other, P * t : P * (t + 1)], ident[:])
+                out_banks.append(out_bank)
+            for t in range(ITEM_TILES):
+                cols = slice(P * t, P * (t + 1))
+                nc.vector.tensor_add(out=mix[:, hop, cols], in0=mix[:, hop, cols], in1=acc["a"][:, cols])
+                nc.tensor.transpose(out_banks[t][:, hop, :], mix[:, hop, cols], ident[:])
+            for t in range(ITEM_TILES):
+                out_sb = out_stage.tile([P, HOPS, D], F32, tag="out_sb", name="out_sb")
+                empty = nc.scalar.copy if t % 2 == 0 else nc.vector.tensor_copy
+                empty(out=out_sb[:], in_=out_banks[t][:])
+                nc.sync.dma_start(out=out_rows[t], in_=out_sb[:])
 
         rounds = [(hop, r) for hop in range(HOPS) for r in range(ROUNDS)]
         for hop, r in rounds[:AHEAD]:
@@ -153,13 +180,3 @@ def tile_dogtaitujuanji_pa_k_kernel(tc, x, w1a, w2a, grad_out, out):
                 multiply_round(*waiting)
             waiting = (hop, operands)
         multiply_round(*waiting)
-
-        out_rows = out.rearrange("(t p) h d -> t p h d", p=P)
-        for t in range(ITEM_TILES):
-            out_bank = bank_pool.tile([P, HOPS, D], F32, tag="bank", name="out_bank")
-            for hop in range(HOPS):
-                nc.tensor.transpose(out_bank[:, hop, :], mix[:, hop, P * t : P * (t + 1)], ident[:])
-            out_sb = out_stage.tile([P, HOPS, D], F32, tag="out_sb", name="out_sb")
-            empty = nc.vector.tensor_copy if t % 2 == 0 else nc.scalar.copy
-            empty(out=out_sb[:], in_=out_bank[:])
-            nc.sync.dma_start(out=out_rows[t], in_=out_sb[:])

@@ -98,7 +98,7 @@ def tile_dogtaitujuanji_pa_k_kernel(tc, x, w1a, w2a, grad_out, out):
                 in_=grouped[:],
             )
 
-        def quantise_round(hop, r):
+        def quantise_round(hop, r, vector_passes):
             operands = []
             for c in range(ROUND_PASSES):
                 grouped = grouped_pool.tile([P, ITEMS * PACK], BF16, align_bytes=64, tag="g_grouped", name="g_grouped")
@@ -108,7 +108,7 @@ def tile_dogtaitujuanji_pa_k_kernel(tc, x, w1a, w2a, grad_out, out):
                     for j in range(2):
                         for u in range(HALVES):
                             transpose_words(bank[:, u, P * j : P * (j + 1)], g_raw[(hop, r, 2 * pair + j)], c, u)
-                    empty = nc.vector.tensor_copy if (c % 2 == 0 and pair == 0) else nc.scalar.copy
+                    empty = nc.vector.tensor_copy if (c in vector_passes and pair == 0) else nc.scalar.copy
                     empty(out=grouped_words[:, 2 * P * pair : 2 * P * (pair + 1), :], in_=bank[:].rearrange("p u n -> p n u"))
                 g_codes = operand_pool.tile([P, ITEMS], U32, align_bytes=64, tag="g_codes", name="g_codes")
                 g_scales = operand_pool.tile([P, ITEMS], U8, align_bytes=64, tag="g_scales", name="g_scales")
@@ -173,7 +173,8 @@ def tile_dogtaitujuanji_pa_k_kernel(tc, x, w1a, w2a, grad_out, out):
                 load_round(*rounds[i + AHEAD])
             if hop == 0:
                 w_grouped = transpose_weights(r)
-            operands = quantise_round(hop, r)
+            vector_passes = {ROUNDS + 1: (0, 1, 2, 3), 2 * ROUNDS + 1: ()}.get(i, (0, 2))
+            operands = quantise_round(hop, r, vector_passes)
             if hop == 0:
                 quantise_weights(r, w_grouped)
             if waiting is not None:

@@ -53,8 +53,8 @@ def tile_dogtaitujuanji_pa_k_kernel(tc, x, w1a, w2a, grad_out, out):
         ident = keep.tile([P, P], F32)
         make_identity(nc, ident[:])
         mix = keep.tile([P, HOPS, ITEMS], F32)
-        w_codes = keep.tile([P, PASSES, 2 * D], U32, align_bytes=64)
-        w_scales = keep.tile([P, PASSES, 2 * D], U8, align_bytes=64)
+        w_codes = keep.tile([P, PASSES, 2 * D], U32, align_bytes=256)
+        w_scales = keep.tile([P, PASSES, 2 * D], U8, align_bytes=256)
 
         g_rows = grad_out.rearrange("(t p) h k -> h t p k", p=P)
         out_rows = out.rearrange("(t p) h d -> t p h d", p=P)
@@ -110,8 +110,8 @@ def tile_dogtaitujuanji_pa_k_kernel(tc, x, w1a, w2a, grad_out, out):
                             transpose_words(bank[:, u, P * j : P * (j + 1)], g_raw[(hop, r, 2 * pair + j)], c, u)
                     empty = nc.vector.tensor_copy if (c in vector_passes and pair == 0) else nc.scalar.copy
                     empty(out=grouped_words[:, 2 * P * pair : 2 * P * (pair + 1), :], in_=bank[:].rearrange("p u n -> p n u"))
-                g_codes = operand_pool.tile([P, ITEMS], U32, align_bytes=64, tag="g_codes", name="g_codes")
-                g_scales = operand_pool.tile([P, ITEMS], U8, align_bytes=64, tag="g_scales", name="g_scales")
+                g_codes = operand_pool.tile([P, ITEMS], U32, align_bytes=256, tag="g_codes", name="g_codes")
+                g_scales = operand_pool.tile([P, ITEMS], U8, align_bytes=256, tag="g_scales", name="g_scales")
                 nc.vector.quantize_mx(out=g_codes[:].bitcast(E5M2_X4), scales=g_scales[:], in_=grouped[:])
                 operands.append((r * ROUND_PASSES + c, g_codes, g_scales))
             return operands

@@ -86,7 +86,7 @@ def tile_dogtaitujuanji_pa_k_kernel(tc, x, w1a, w2a, grad_out, out):
                 for which in range(2):
                     for u in range(HALVES):
                         transpose_words(bank[:, u, D * which : D * (which + 1)], w_raw[(which, r)], c, u)
-                empty = nc.vector.tensor_copy if c % 2 == 0 else nc.scalar.copy
+                empty = nc.vector.tensor_copy if c == 0 else nc.scalar.copy
                 empty(out=grouped_words[:, c, :, :], in_=bank[:].rearrange("p u m -> p m u"))
             return grouped
 

@@ -26,7 +26,6 @@ ROUND_K = ROUND_PASSES * K_PASS
 ROUNDS = PASSES // ROUND_PASSES
 AHEAD = 5
 BANKS = 6
-WARM_UP = 4
 
 FLOPS = 2 * 2 * ITEMS * HOPS * E * D
 BYTES = 2 * ITEMS * HOPS * E + 2 * 2 * D * E + 4 * ITEMS * HOPS * D
@@ -45,11 +44,6 @@ def tile_dogtaitujuanji_pa_k_kernel(tc, x, w1a, w2a, grad_out, out):
         acc_pool = ctx.enter_context(tc.psum_pool(name="acc", bufs=1))
         bank_pool = ctx.enter_context(tc.psum_pool(name="banks", bufs=BANKS))
 
-        zeros = keep.tile([P, ITEMS], BF16)
-        nc.vector.memset(zeros[:], 0.0)
-        warm_bank = bank_pool.tile([P, ITEMS], F32, tag="bank", name="warm_bank")
-        for i in range(WARM_UP):
-            nc.tensor.matmul(warm_bank[:], lhsT=zeros[:, :P], rhs=zeros[:], start=True, stop=True)
         ident = keep.tile([P, P], F32)
         make_identity(nc, ident[:])
         mix = keep.tile([P, HOPS, ITEMS], F32)

from contextlib import ExitStack

import concourse.mybir as mybir
from concourse.masks import make_identity

F32 = mybir.dt.float32
BF16 = mybir.dt.bfloat16
U32 = mybir.dt.uint32
U8 = mybir.dt.uint8
E5M2_X4 = mybir.dt.float8_e5m2_x4
E4M3_X4 = mybir.dt.float8_e4m3fn_x4
MULT = mybir.AluOpType.mult
ADD = mybir.AluOpType.add
COPY = mybir.ActivationFunctionType.Copy

ITEMS, HOPS, D, E = 512, 3, 128, 8192
P = 128
PACK = 4
K_PASS = P * PACK
PASSES = E // K_PASS
HALVES = 2
WORDS = K_PASS // 2
ITEM_TILES = ITEMS // P
ROUND_PASSES = 4
ROUND_K = ROUND_PASSES * K_PASS
ROUNDS = PASSES // ROUND_PASSES
AHEAD = 5
BANKS = 6

FLOPS = 2 * 2 * ITEMS * HOPS * E * D
BYTES = 2 * ITEMS * HOPS * E + 2 * 2 * D * E + 4 * ITEMS * HOPS * D


def tile_dogtaitujuanji_pa_k_kernel(tc, x, w1a, w2a, grad_out, out):
    nc = tc.nc
    with ExitStack() as ctx:
        keep = ctx.enter_context(tc.tile_pool(name="keep", bufs=1))
        w_raw_pool = ctx.enter_context(tc.tile_pool(name="w_raw", bufs=2 * ROUNDS))
        g_raw_pool = ctx.enter_context(tc.tile_pool(name="g_raw", bufs=ITEM_TILES * (AHEAD + 1)))
        grouped_pool = ctx.enter_context(tc.tile_pool(name="grouped", bufs=ROUND_PASSES))
        w_grouped_pool = ctx.enter_context(tc.tile_pool(name="w_grouped", bufs=2))
        operand_pool = ctx.enter_context(tc.tile_pool(name="operands", bufs=2 * ROUND_PASSES))
        out_stage = ctx.enter_context(tc.tile_pool(name="out_stage", bufs=ITEM_TILES))
        acc_pool = ctx.enter_context(tc.psum_pool(name="acc", bufs=1))
        bank_pool = ctx.enter_context(tc.psum_pool(name="banks", bufs=BANKS))

        ident = keep.tile([P, P], F32)
        make_identity(nc, ident[:])
        mix = keep.tile([P, HOPS, ITEMS], F32)
        w_codes = keep.tile([P, PASSES, 2 * D], U32, align_bytes=256)
        w_scales = keep.tile([P, PASSES, 2 * D], U8, align_bytes=256)

        g_rows = grad_out.rearrange("(t p) h k -> h t p k", p=P)
        out_rows = out.rearrange("(t p) h d -> t p h d", p=P)
        w_raw = {}
        g_raw = {}
        acc = {}

        def load_round(hop, r):
            k_cols = slice(r * ROUND_K, (r + 1) * ROUND_K)
            if hop == 0:
                for which, w in enumerate((w2a, w1a)):
                    w_piece = w_raw_pool.tile([P, ROUND_K], BF16, tag="w_raw", name="w_piece")
                    nc.sync.dma_start(out=w_piece[:], in_=w[:, k_cols])
                    w_raw[(which, r)] = w_piece
            for t in range(ITEM_TILES):
                g_piece = g_raw_pool.tile([P, ROUND_K], BF16, tag="g_raw", name="g_piece")
                nc.sync.dma_start(out=g_piece[:], in_=g_rows[hop, t, :, k_cols])
                g_raw[(hop, r, t)] = g_piece

        def transpose_words(bank_cols, piece, c, u):
            first = WORDS * c + P * u
            nc.tensor.transpose(bank_cols, piece[:].bitcast(F32)[:, first : first + P], ident[:])

        def transpose_weights(r):
            grouped = w_grouped_pool.tile([P, ROUND_PASSES * 2 * D * PACK], BF16, align_bytes=64, tag="w_grouped", name="w_grouped")
            grouped_words = grouped[:].bitcast(F32).rearrange("p (c m u) -> p c m u", c=ROUND_PASSES, u=HALVES)
            for c in range(ROUND_PASSES):
                bank = bank_pool.tile([P, HALVES, 2 * D], F32, tag="bank", name="w_bank")
                for which in range(2):
                    for u in range(HALVES):
                        transpose_words(bank[:, u, D * which : D * (which + 1)], w_raw[(which, r)], c, u)
                empty = nc.vector.tensor_copy if c == 0 else nc.scalar.copy
                empty(out=grouped_words[:, c, :, :], in_=bank[:].rearrange("p u m -> p m u"))
            return grouped

        def quantise_weights(r, grouped):
            passes = slice(r * ROUND_PASSES, (r + 1) * ROUND_PASSES)
            nc.vector.quantize_mx(
                out=w_codes[:, passes, :].rearrange("p c m -> p (c m)").bitcast(E4M3_X4),
                scales=w_scales[:, passes, :].rearrange("p c m -> p (c m)"),
                in_=grouped[:],
            )

        def quantise_round(hop, r, vector_passes):
            operands = []
            for c in range(ROUND_PASSES):
                grouped = grouped_pool.tile([P, ITEMS * PACK], BF16, align_bytes=64, tag="g_grouped", name="g_grouped")
                grouped_words = grouped[:].bitcast(F32).rearrange("p (n u) -> p n u", u=HALVES)
                for pair in range(ITEM_TILES // 2):
                    bank = bank_pool.tile([P, HALVES, 2 * P], F32, tag="bank", name="g_bank")
                    for j in range(2):
                        for u in range(HALVES):
                            transpose_words(bank[:, u, P * j : P * (j + 1)], g_raw[(hop, r, 2 * pair + j)], c, u)
                    empty = nc.vector.tensor_copy if (c in vector_passes and pair == 0) else nc.scalar.copy
                    empty(out=grouped_words[:, 2 * P * pair : 2 * P * (pair + 1), :], in_=bank[:].rearrange("p u n -> p n u"))
                g_codes = operand_pool.tile([P, ITEMS], U32, align_bytes=256, tag="g_codes", name="g_codes")
                g_scales = operand_pool.tile([P, ITEMS], U8, align_bytes=256, tag="g_scales", name="g_scales")
                nc.vector.quantize_mx(out=g_codes[:].bitcast(E5M2_X4), scales=g_scales[:], in_=grouped[:])
                operands.append((r * ROUND_PASSES + c, g_codes, g_scales))
            return operands

        def multiply_round(hop, operands):
            if operands[0][0] == 0:
                acc["a"] = acc_pool.tile([P, ITEMS], F32, tag="acc_a", name="acc_a")
                acc["b"] = acc_pool.tile([P, ITEMS], F32, tag="acc_b", name="acc_b")
            for key, which in (("b", 1), ("a", 0)):
                for c, g_codes, g_scales in operands:
                    nc.tensor.matmul_mx(
                        out=acc[key][:],
                        lhsT=w_codes[:, c, D * which : D * (which + 1)].bitcast(E4M3_X4),
                        lhsT_scale=w_scales[:, c, D * which : D * (which + 1)],
                        rhs=g_codes[:].bitcast(E5M2_X4),
                        rhs_scale=g_scales[:],
                        start=(c == 0),
                        stop=(c == PASSES - 1),
                    )
            if operands[-1][0] == PASSES - 1:
                finish_hop(hop)

        def finish_hop(hop):
            others = [other for other in range(HOPS) if other != hop]
            if hop == 0:
                for other in others:
                    nc.scalar.activation(out=mix[:, other, :], in_=acc["b"][:], func=COPY, scale=0.5)
                nc.scalar.copy(out=mix[:, hop, :], in_=acc["a"][:])
                return
            for other in others:
                nc.vector.scalar_tensor_tensor(
                    out=mix[:, other, :], in0=acc["b"][:], scalar=0.5, in1=mix[:, other, :], op0=MULT, op1=ADD
                )
            if hop < HOPS - 1:
                nc.vector.tensor_add(out=mix[:, hop, :], in0=mix[:, hop, :], in1=acc["a"][:])
                return
            out_banks = []
            for t in range(ITEM_TILES):
                out_bank = bank_pool.tile([P, HOPS, D], F32, tag="bank", name="out_bank")
                for other in others:
                    nc.tensor.transpose(out_bank[:, other, :], mix[:, other, P * t : P * (t + 1)], ident[:])
                out_banks.append(out_bank)
            for t in range(ITEM_TILES):
                cols = slice(P * t, P * (t + 1))
                nc.vector.tensor_add(out=mix[:, hop, cols], in0=mix[:, hop, cols], in1=acc["a"][:, cols])
                nc.tensor.transpose(out_banks[t][:, hop, :], mix[:, hop, cols], ident[:])
            for t in range(ITEM_TILES):
                out_sb = out_stage.tile([P, HOPS, D], F32, tag="out_sb", name="out_sb")
                empty = nc.scalar.copy if t % 2 == 0 else nc.vector.tensor_copy
                empty(out=out_sb[:], in_=out_banks[t][:])
                nc.sync.dma_start(out=out_rows[t], in_=out_sb[:])

        rounds = [(hop, r) for hop in range(HOPS) for r in range(ROUNDS)]
        for hop, r in rounds[:AHEAD]:
            load_round(hop, r)
        waiting = None
        for i, (hop, r) in enumerate(rounds):
            if i + AHEAD < len(rounds):
                load_round(*rounds[i + AHEAD])
            if hop == 0:
                w_grouped = transpose_weights(r)
            vector_passes = {ROUNDS + 1: (0, 1, 2, 3), 2 * ROUNDS + 1: ()}.get(i, (0, 2))
            operands = quantise_round(hop, r, vector_passes)
            if hop == 0:
                quantise_weights(r, w_grouped)
            if waiting is not None:
                multiply_round(*waiting)
            waiting = (hop, operands)
        multiply_round(*waiting)
